import numpy as np
import ml_dtypes


def mxq(x, axis, fmt="e4m3"):
    dtype, down = {"e4m3": (ml_dtypes.float8_e4m3fn, 7), "e5m2": (ml_dtypes.float8_e5m2, 14)}[fmt]
    v = np.moveaxis(np.asarray(x, np.float32).astype(ml_dtypes.bfloat16).astype(np.float64), axis, -1)
    blocks = v.reshape(v.shape[:-1] + (-1, 32))
    amax = np.abs(blocks).max(-1, keepdims=True)
    byte = np.maximum(np.where(amax > 0, np.frexp(amax)[1] - 1 + 127, 0) - down, 1)
    scale = np.exp2(byte - 127.0)
    codes = (blocks / scale).astype(np.float32).astype(dtype).astype(np.float64)
    return np.moveaxis((codes * scale).reshape(v.shape), -1, axis)


WIDE = False


def mx_kscale(k):
    if not WIDE:
        return np.ones(k)
    levels = np.array([10, -10, 5, -5, 0])
    if k % 512:
        return np.exp2(np.random.permutation(np.resize(levels, k // 32))).repeat(32)
    a = np.empty((k // 512, 16))
    for p in range(k // 512):
        a[p, :8] = np.random.permutation(np.resize(levels, 8))
        for g in range(8):
            far = levels[np.abs(levels - a[p, g]) >= 10]
            a[p, g + 8] = far[np.random.randint(len(far))]
    return np.exp2(a.ravel()).repeat(32)


BF16 = ml_dtypes.bfloat16


def bf(x):
    return np.asarray(x, np.float32).astype(BF16)


def f64(x):
    return np.asarray(x).astype(np.float64)


B, S, IQ, OQ, Q = 4, 256, 512, 512, 4


def setup_inputs():
    s = mx_kscale(IQ)
    sw = 0.5 / np.sqrt(IQ)
    return {"x": bf((np.random.standard_normal((B, S, IQ, Q)) * s[:, None]).reshape(B, S, IQ * Q)),
            "wr": bf(np.random.standard_normal((OQ, IQ)) * sw / s),
            "wi": bf(np.random.standard_normal((OQ, IQ)) * sw / s),
            "wj": bf(np.random.standard_normal((OQ, IQ)) * sw / s),
            "wk": bf(np.random.standard_normal((OQ, IQ)) * sw / s),
            "bias": bf(np.random.standard_normal(OQ * Q) * 0.3)}


def reference(x, wr, wi, wj, wk, bias):
    xq = f64(x).reshape(B * S, IQ, Q)
    xr = mxq(xq[:, :, 0], 1, "e4m3")
    xi = mxq(xq[:, :, 1], 1, "e4m3")
    xj = mxq(xq[:, :, 2], 1, "e4m3")
    xk = mxq(xq[:, :, 3], 1, "e4m3")
    qr = mxq(f64(wr), 1, "e4m3")
    qi = mxq(f64(wi), 1, "e4m3")
    qj = mxq(f64(wj), 1, "e4m3")
    qk = mxq(f64(wk), 1, "e4m3")
    Ar = xr @ qr.T
    Br = xi @ qr.T
    Cr = xj @ qr.T
    Dr = xk @ qr.T
    Ai = xr @ qi.T
    Bi = xi @ qi.T
    Aj = xr @ qj.T
    Cj = xj @ qj.T
    Ak = xr @ qk.T
    Dk = xk @ qk.T
    or_ = Ar - Bi - Cj - Dk
    oi_ = Br + Ai + Dk - Cj
    oj_ = Cr - Dk + Aj + Bi
    ok_ = Dr + Cj - Bi + Ak
    out = np.stack([or_, oi_, oj_, ok_], axis=-1).reshape(B, S, Q * OQ)
    return out + f64(bias)[None, None, :]

@@ -1,0 +1,217 @@
+import concourse.mybir as mybir
+from concourse.masks import make_identity
+
+F32 = mybir.dt.float32
+BF16 = mybir.dt.bfloat16
+U32 = mybir.dt.uint32
+U8 = mybir.dt.uint8
+FP8X4 = mybir.dt.float8_e4m3fn_x4
+
+P = 128
+Q = 4
+ROWS = 1024
+IQ = 512
+OQ = 512
+ROW_TILES = ROWS // P
+PAIRS = ROW_TILES // 2
+O_BLOCKS = OQ // P
+MATRIX = P * 4
+BANK_BF16 = 1024
+MATMUL_COLS = 512
+DEINTERLEAVE_AT = 0
+TRANSPOSE_AT = 2
+SHARED = 2
+
+FLOPS = 2 * ROWS * IQ * OQ * 10
+
+WR = 0
+WI = 1
+WJ = 2
+WK = 3
+NEG_WI = 4
+NEG_WJ = 5
+NEG_WK = 6
+SIGNED = 7
+
+WEIGHT_FOR = (
+    (WR, NEG_WI, NEG_WJ, NEG_WK),
+    (WI, WR, NEG_WJ, WK),
+    (WJ, WI, WR, NEG_WK),
+    (WK, NEG_WI, WJ, WR),
+)
+
+ROW_OF_BLOCKS = (NEG_WK, WR, WI, NEG_WI, WR, WJ, WK, NEG_WK, WK, NEG_WJ, NEG_WJ)
+SERVED = 2
+SLOTS = len(ROW_OF_BLOCKS)
+
+
+def slot_of(wanted):
+    for s in range(SLOTS - SERVED + 1):
+        if ROW_OF_BLOCKS[s : s + SERVED] == wanted:
+            return s
+    raise AssertionError("these weights are not neighbours in ROW_OF_BLOCKS")
+
+
+def tile_quaternionlinear_pa_kernel(tc, x, wr, wi, wj, wk, bias, out):
+    nc = tc.nc
+    x_rows = x.flatten_outer_dims()
+    out_rows = out.flatten_outer_dims()
+    weights = (wr, wi, wj, wk)
+
+    with tc.tile_pool(name="keep", bufs=1) as keep, tc.tile_pool(name="stage", bufs=4) as stage, tc.tile_pool(
+        name="results", bufs=4
+    ) as results, tc.psum_pool(name="flipped", bufs=4) as flipped, tc.psum_pool(name="sums", bufs=4) as sums, tc.manual_schedule():
+        bias_row = keep.tile([P, OQ * Q], BF16)
+        nc.vector.memset(bias_row[:], 0.0)
+        nc.scalar.dma_start(out=bias_row[0:1, :], in_=bias.unsqueeze(0))
+        ones = keep.tile([P, P], BF16)
+        nc.vector.memset(ones[:], 1.0)
+
+        w_raw = {}
+        x_raw = {}
+
+        def load_weights(ob):
+            block = keep.tile([P, Q, IQ], BF16, name="w_raw%d" % ob)
+            for m in range(Q):
+                nc.sync.dma_start(out=block[:, m, :], in_=weights[m][ob * P : (ob + 1) * P, :])
+            w_raw[ob] = block
+
+        def load_x(t):
+            rows = keep.tile([P, IQ * Q], BF16, name="x_raw%d" % t)
+            nc.sync.dma_start(out=rows[:], in_=x_rows[t * P : (t + 1) * P, :])
+            x_raw[t] = rows
+
+        load_weights(0)
+        load_x(0)
+        load_x(1)
+        for ob in range(1, O_BLOCKS):
+            load_weights(ob)
+        for t in range(2, ROW_TILES):
+            load_x(t)
+
+        identity = keep.tile([P, P], F32)
+        make_identity(nc, identity[:])
+
+        w_codes = keep.tile([P, O_BLOCKS, SLOTS * P], U32, align_bytes=64)
+        w_scales = keep.tile([P, O_BLOCKS, SLOTS * P], U8, align_bytes=64)
+        x_codes = keep.tile([P, ROW_TILES, Q * P], U32, align_bytes=64)
+        x_scales = keep.tile([P, ROW_TILES, Q * P], U8, align_bytes=64)
+        bias_all = keep.tile([P, OQ * Q], BF16)
+        planes = {}
+        x_grouped = {}
+        w_signed = {}
+
+        def spread_bias():
+            for b in range(OQ * Q // BANK_BF16):
+                bank = flipped.tile([P, BANK_BF16], BF16, tag="bank")
+                for h in range(BANK_BF16 // MATMUL_COLS):
+                    nc.tensor.matmul(
+                        out=bank[:, h * MATMUL_COLS : (h + 1) * MATMUL_COLS],
+                        lhsT=ones[:],
+                        rhs=bias_row[:, b * BANK_BF16 + h * MATMUL_COLS : b * BANK_BF16 + (h + 1) * MATMUL_COLS],
+                        start=True,
+                        stop=True,
+                    )
+                nc.scalar.copy(out=bias_all[:, b * BANK_BF16 : (b + 1) * BANK_BF16], in_=bank[:])
+
+        def transpose_and_group(four, grouped):
+            words = four.bitcast(F32).rearrange("r m (p u) -> r m u p", u=2)
+            grouped_words = grouped.bitcast(F32).rearrange("p (m r u) -> p m r u", m=Q, u=2)
+            for pair in range(2):
+                bank = flipped.tile([P, 2, 2, P], F32, tag="bank")
+                for m in range(2):
+                    for u in range(2):
+                        nc.tensor.transpose(bank[:, m, u, :], words[:, 2 * pair + m, u, :], identity[:])
+                nc.scalar.copy(
+                    out=grouped_words[:, 2 * pair : 2 * pair + 2, :, :], in_=bank[:].rearrange("p m u r -> p m r u")
+                )
+
+        def transpose_weights(ob):
+            signed = stage.tile([P, SIGNED * MATRIX], BF16, align_bytes=64)
+            transpose_and_group(w_raw[ob][:], signed[:, 0 : Q * MATRIX])
+            w_signed[ob] = signed
+
+        def quantise_weights(ob):
+            signed = w_signed[ob]
+            nc.vector.tensor_scalar(
+                out=signed[:, NEG_WI * MATRIX :],
+                in0=signed[:, WI * MATRIX : Q * MATRIX],
+                scalar1=-1.0,
+                scalar2=None,
+                op0=mybir.AluOpType.mult,
+            )
+            for negated in (False, True):
+                for s in range(SLOTS):
+                    which = ROW_OF_BLOCKS[s]
+                    if (which >= NEG_WI) == negated:
+                        nc.vector.quantize_mx(
+                            out=w_codes[:, ob, s * P : (s + 1) * P].bitcast(FP8X4),
+                            scales=w_scales[:, ob, s * P : (s + 1) * P],
+                            in_=signed[:, which * MATRIX : (which + 1) * MATRIX],
+                        )
+
+        def deinterleave(t, on_vector):
+            separate = stage.tile([P, Q, IQ], BF16)
+            interleaved = x_raw[t][:].rearrange("p (i c) -> p c i", c=Q)
+            nc.vector.tensor_copy(out=separate[:, 0:on_vector, :], in_=interleaved[:, 0:on_vector, :])
+            if on_vector < Q:
+                nc.scalar.copy(out=separate[:, on_vector:Q, :], in_=interleaved[:, on_vector:Q, :])
+            planes[t] = separate
+
+        def transpose_x(t):
+            grouped = stage.tile([P, Q * MATRIX], BF16, align_bytes=64)
+            transpose_and_group(planes[t][:], grouped[:])
+            x_grouped[t] = grouped
+
+        def quantise_x(t):
+            nc.vector.quantize_mx(out=x_codes[:, t, :].bitcast(FP8X4), scales=x_scales[:, t, :], in_=x_grouped[t][:])
+
+        def multiply(t, ob):
+            acc = sums.tile([P, Q * P], F32)
+            for first in range(0, Q, SERVED):
+                for c_in in range(Q):
+                    s = slot_of(tuple(WEIGHT_FOR[c_out][c_in] for c_out in range(first, first + SERVED)))
+                    nc.tensor.matmul_mx(
+                        out=acc[:, first * P : (first + SERVED) * P],
+                        lhsT=x_codes[:, t, c_in * P : (c_in + 1) * P].bitcast(FP8X4),
+                        lhsT_scale=x_scales[:, t, c_in * P : (c_in + 1) * P],
+                        rhs=w_codes[:, ob, s * P : (s + SERVED) * P].bitcast(FP8X4),
+                        rhs_scale=w_scales[:, ob, s * P : (s + SERVED) * P],
+                        start=(c_in == 0),
+                        stop=(c_in == Q - 1),
+                    )
+            cols = slice(ob * P * Q, (ob + 1) * P * Q)
+            result = results.tile([P, P * Q], F32)
+            nc.vector.tensor_tensor(
+                out=result[:].rearrange("p (o c) -> p o c", c=Q),
+                in0=acc[:].rearrange("p (c o) -> p o c", c=Q),
+                in1=bias_all[:, cols].rearrange("p (o c) -> p o c", c=Q),
+                op=mybir.AluOpType.add,
+            )
+            nc.sync.dma_start(out=out_rows[t * P : (t + 1) * P, cols], in_=result[:])
+
+        transpose_weights(0)
+        spread_bias()
+        deinterleave(0, Q)
+        transpose_x(0)
+        deinterleave(1, Q)
+        quantise_weights(0)
+        quantise_x(0)
+        transpose_x(1)
+        quantise_x(1)
+
+        for pair in range(PAIRS):
+            here = (2 * pair, 2 * pair + 1)
+            ahead = (2 * pair + 2, 2 * pair + 3) if pair + 1 < PAIRS else ()
+            for ob in range(O_BLOCKS):
+                if pair == 0 and ob + 1 < O_BLOCKS:
+                    transpose_weights(ob + 1)
+                    quantise_weights(ob + 1)
+                for t in ahead:
+                    if ob == DEINTERLEAVE_AT:
+                        deinterleave(t, SHARED)
+                    if ob == TRANSPOSE_AT:
+                        transpose_x(t)
+                        quantise_x(t)
+                for t in here:
+                    multiply(t, ob)

@@ -114,8 +114,7 @@ def tile_quaternionlinear_pa_kernel(tc, x, wr, wi, wj, wk, bias, out):
                     )
                 nc.scalar.copy(out=bias_all[:, b * BANK_BF16 : (b + 1) * BANK_BF16], in_=bank[:])
 
-        def transpose_and_group(four, grouped):
-            words = four.bitcast(F32).rearrange("r m (p u) -> r m u p", u=2)
+        def transpose_and_group(words, grouped):
             grouped_words = grouped.bitcast(F32).rearrange("p (m r u) -> p m r u", m=Q, u=2)
             for pair in range(2):
                 bank = flipped.tile([P, 2, 2, P], F32, tag="bank")
@@ -128,7 +127,9 @@ def tile_quaternionlinear_pa_kernel(tc, x, wr, wi, wj, wk, bias, out):
 
         def transpose_weights(ob):
             signed = stage.tile([P, SIGNED * MATRIX], BF16, align_bytes=64)
-            transpose_and_group(w_raw[ob][:], signed[:, 0 : Q * MATRIX])
+            transpose_and_group(
+                w_raw[ob][:].bitcast(F32).rearrange("r m (p u) -> r m u p", u=2), signed[:, 0 : Q * MATRIX]
+            )
             w_signed[ob] = signed
 
         def quantise_weights(ob):
@@ -151,16 +152,17 @@ def tile_quaternionlinear_pa_kernel(tc, x, wr, wi, wj, wk, bias, out):
                         )
 
         def deinterleave(t, on_vector):
-            separate = stage.tile([P, Q, IQ], BF16)
-            interleaved = x_raw[t][:].rearrange("p (i c) -> p c i", c=Q)
-            nc.vector.tensor_copy(out=separate[:, 0:on_vector, :], in_=interleaved[:, 0:on_vector, :])
+            separate = stage.tile([P, Q, 2, P, 2], BF16)
+            interleaved = x_raw[t][:].rearrange("r (p u e c) -> r c u p e", u=2, e=2, c=Q)
+            nc.vector.tensor_copy(out=separate[:, 0:on_vector], in_=interleaved[:, 0:on_vector])
             if on_vector < Q:
-                nc.scalar.copy(out=separate[:, on_vector:Q, :], in_=interleaved[:, on_vector:Q, :])
+                nc.scalar.copy(out=separate[:, on_vector:Q], in_=interleaved[:, on_vector:Q])
             planes[t] = separate
 
         def transpose_x(t):
             grouped = stage.tile([P, Q * MATRIX], BF16, align_bytes=64)
-            transpose_and_group(planes[t][:], grouped[:])
+            words = planes[t][:].rearrange("r m u p e -> r m (u p e)").bitcast(F32)
+            transpose_and_group(words.rearrange("r m (u p) -> r m u p", u=2), grouped[:])
             x_grouped[t] = grouped
 
         def quantise_x(t):

@@ -17,6 +17,8 @@ PAIRS = ROW_TILES // 2
 O_BLOCKS = OQ // P
 MATRIX = P * 4
 BANK_BF16 = 1024
+BLOCK = 32
+BLOCKS = P // BLOCK
 MATMUL_COLS = 512
 DEINTERLEAVE_AT = 0
 TRANSPOSE_AT = 2
@@ -61,11 +63,12 @@ def tile_quaternionlinear_pa_kernel(tc, x, wr, wi, wj, wk, bias, out):
     with tc.tile_pool(name="keep", bufs=1) as keep, tc.tile_pool(name="stage", bufs=4) as stage, tc.tile_pool(
         name="results", bufs=4
     ) as results, tc.psum_pool(name="flipped", bufs=4) as flipped, tc.psum_pool(name="sums", bufs=4) as sums, tc.manual_schedule():
-        bias_row = keep.tile([P, OQ * Q], BF16)
-        nc.vector.memset(bias_row[:], 0.0)
-        nc.scalar.dma_start(out=bias_row[0:1, :], in_=bias.unsqueeze(0))
         ones = keep.tile([P, P], BF16)
         nc.vector.memset(ones[:], 1.0)
+        table_load = keep.tile([P, 1], BF16)
+        nc.scalar.copy(out=table_load[:], in_=ones[:, 0:1])
+        bias_row = keep.tile([P, OQ * Q], BF16)
+        nc.vector.memset(bias_row[:].bitcast(U32), 0)
 
         w_raw = {}
         x_raw = {}
@@ -81,13 +84,25 @@ def tile_quaternionlinear_pa_kernel(tc, x, wr, wi, wj, wk, bias, out):
             nc.sync.dma_start(out=rows[:], in_=x_rows[t * P : (t + 1) * P, :])
             x_raw[t] = rows
 
+        def load_x_by_quarters(t):
+            rows = keep.tile([P, BLOCKS, IQ], BF16, name="x_raw%d" % t)
+            for q in (0, 2, 1, 3):
+                nc.sync.dma_start(
+                    out=rows[q * BLOCK : (q + 1) * BLOCK, :, :],
+                    in_=x_rows[t * P : (t + 1) * P, q * IQ : (q + 1) * IQ].rearrange("(n r) w -> r n w", n=BLOCKS),
+                )
+            x_raw[t] = rows
+
         load_weights(0)
         load_x(0)
+        nc.sync.dma_start(out=bias_row[0:1, :], in_=bias.unsqueeze(0))
         load_x(1)
         for ob in range(1, O_BLOCKS):
             load_weights(ob)
-        for t in range(2, ROW_TILES):
-            load_x(t)
+        load_x(2)
+        load_x(3)
+        for t in range(4, ROW_TILES):
+            load_x_by_quarters(t)
 
         identity = keep.tile([P, P], F32)
         make_identity(nc, identity[:])
@@ -99,6 +114,7 @@ def tile_quaternionlinear_pa_kernel(tc, x, wr, wi, wj, wk, bias, out):
         bias_all = keep.tile([P, OQ * Q], BF16)
         planes = {}
         x_grouped = {}
+        accs = {}
         w_signed = {}
 
         def spread_bias():
@@ -168,8 +184,30 @@ def tile_quaternionlinear_pa_kernel(tc, x, wr, wi, wj, wk, bias, out):
         def quantise_x(t):
             nc.vector.quantize_mx(out=x_codes[:, t, :].bitcast(FP8X4), scales=x_scales[:, t, :], in_=x_grouped[t][:])
 
+        def deinterleave_quarters(t):
+            blocks = stage.tile([P, BLOCKS, Q, 2, BLOCK, 2], BF16, align_bytes=64)
+            source = x_raw[t][:].rearrange("p n (a u e c) -> p c n u a e", u=2, e=2, c=Q)
+            target = blocks[:].rearrange("p n c u a e -> p c n u a e")
+            for c in range(Q):
+                nc.scalar.copy(out=target[:, c], in_=source[:, c])
+            planes[t] = blocks
+
+        def transpose_blocks(t):
+            turned = stage.tile([P, BLOCKS * Q * 2 * BLOCK], F32, align_bytes=64)
+            nc.vector.transpose(turned[:], planes[t][:].rearrange("p n c u a e -> p (n c u a e)").bitcast(F32))
+            planes[t] = turned
+
+        def group_blocks(t):
+            grouped = stage.tile([P, Q * MATRIX], BF16, align_bytes=64)
+            nc.scalar.copy(
+                out=grouped[:].bitcast(F32).rearrange("p (c n r u) -> p c n r u", c=Q, n=BLOCKS, u=2),
+                in_=planes[t][:].rearrange("p (n c u r) -> p c n r u", n=BLOCKS, c=Q, u=2),
+            )
+            x_grouped[t] = grouped
+
         def multiply(t, ob):
             acc = sums.tile([P, Q * P], F32)
+            accs[t, ob] = acc
             for first in range(0, Q, SERVED):
                 for c_in in range(Q):
                     s = slot_of(tuple(WEIGHT_FOR[c_out][c_in] for c_out in range(first, first + SERVED)))
@@ -182,6 +220,9 @@ def tile_quaternionlinear_pa_kernel(tc, x, wr, wi, wj, wk, bias, out):
                         start=(c_in == 0),
                         stop=(c_in == Q - 1),
                     )
+
+        def finish(t, ob):
+            acc = accs[t, ob]
             cols = slice(ob * P * Q, (ob + 1) * P * Q)
             result = results.tile([P, P * Q], F32)
             nc.vector.tensor_tensor(
@@ -193,7 +234,6 @@ def tile_quaternionlinear_pa_kernel(tc, x, wr, wi, wj, wk, bias, out):
             nc.sync.dma_start(out=out_rows[t * P : (t + 1) * P, cols], in_=result[:])
 
         transpose_weights(0)
-        spread_bias()
         deinterleave(0, Q)
         transpose_x(0)
         deinterleave(1, Q)
@@ -202,18 +242,39 @@ def tile_quaternionlinear_pa_kernel(tc, x, wr, wi, wj, wk, bias, out):
         transpose_x(1)
         quantise_x(1)
 
-        for pair in range(PAIRS):
-            here = (2 * pair, 2 * pair + 1)
-            ahead = (2 * pair + 2, 2 * pair + 3) if pair + 1 < PAIRS else ()
+        for ob in range(O_BLOCKS):
+            if ob + 1 < O_BLOCKS:
+                transpose_weights(ob + 1)
+                quantise_weights(ob + 1)
+            for t in (2, 3):
+                if ob == DEINTERLEAVE_AT:
+                    deinterleave(t, SHARED)
+                if ob == TRANSPOSE_AT:
+                    transpose_x(t)
+                    quantise_x(t)
+            for t in (0, 1):
+                multiply(t, ob)
+            if ob == 0:
+                spread_bias()
+            for t in (0, 1):
+                finish(t, ob)
+
+        for pair in range(1, PAIRS):
+            a, b = 2 * pair + 2, 2 * pair + 3
+            ahead = (
+                ((deinterleave_quarters, a),),
+                ((deinterleave_quarters, b),),
+                (),
+                ((transpose_blocks, a),),
+                ((group_blocks, a),),
+                ((transpose_blocks, b),),
+                ((group_blocks, b), (quantise_x, a)),
+                ((quantise_x, b),),
+            )
             for ob in range(O_BLOCKS):
-                if pair == 0 and ob + 1 < O_BLOCKS:
-                    transpose_weights(ob + 1)
-                    quantise_weights(ob + 1)
-                for t in ahead:
-                    if ob == DEINTERLEAVE_AT:
-                        deinterleave(t, SHARED)
-                    if ob == TRANSPOSE_AT:
-                        transpose_x(t)
-                        quantise_x(t)
-                for t in here:
+                for t in (2 * pair, 2 * pair + 1):
+                    if pair + 1 < PAIRS:
+                        for step, tile in ahead[2 * ob + t % 2]:
+                            step(tile)
                     multiply(t, ob)
+                    finish(t, ob)

@@ -61,9 +61,9 @@ def tile_quaternionlinear_pa_kernel(tc, x, wr, wi, wj, wk, bias, out):
     weights = (wr, wi, wj, wk)
 
     with tc.tile_pool(name="keep", bufs=1) as keep, tc.tile_pool(name="stage", bufs=4) as stage, tc.tile_pool(
-        name="results", bufs=4
+        name="results", bufs=8
     ) as results, tc.psum_pool(name="flipped", bufs=4) as flipped, tc.psum_pool(name="sums", bufs=4) as sums, tc.manual_schedule():
-        ones = keep.tile([P, P], BF16)
+        ones = keep.tile([P, MATMUL_COLS], BF16)
         nc.vector.memset(ones[:], 1.0)
         table_load = keep.tile([P, 1], BF16)
         nc.scalar.copy(out=table_load[:], in_=ones[:, 0:1])
@@ -117,13 +117,18 @@ def tile_quaternionlinear_pa_kernel(tc, x, wr, wi, wj, wk, bias, out):
         accs = {}
         w_signed = {}
 
+        def keep_warm(n):
+            unread = sums.tile([P, MATMUL_COLS], F32, tag="acc")
+            for i in range(n):
+                nc.tensor.matmul(out=unread[:], lhsT=ones[:, 0:P], rhs=ones[:], start=True, stop=True)
+
         def spread_bias():
             for b in range(OQ * Q // BANK_BF16):
                 bank = flipped.tile([P, BANK_BF16], BF16, tag="bank")
                 for h in range(BANK_BF16 // MATMUL_COLS):
                     nc.tensor.matmul(
                         out=bank[:, h * MATMUL_COLS : (h + 1) * MATMUL_COLS],
-                        lhsT=ones[:],
+                        lhsT=ones[:, 0:P],
                         rhs=bias_row[:, b * BANK_BF16 + h * MATMUL_COLS : b * BANK_BF16 + (h + 1) * MATMUL_COLS],
                         start=True,
                         stop=True,
@@ -206,7 +211,7 @@ def tile_quaternionlinear_pa_kernel(tc, x, wr, wi, wj, wk, bias, out):
             x_grouped[t] = grouped
 
         def multiply(t, ob):
-            acc = sums.tile([P, Q * P], F32)
+            acc = sums.tile([P, Q * P], F32, tag="acc")
             accs[t, ob] = acc
             for first in range(0, Q, SERVED):
                 for c_in in range(Q):
@@ -233,13 +238,17 @@ def tile_quaternionlinear_pa_kernel(tc, x, wr, wi, wj, wk, bias, out):
             )
             nc.sync.dma_start(out=out_rows[t * P : (t + 1) * P, cols], in_=result[:])
 
+        keep_warm(4)
         transpose_weights(0)
+        keep_warm(6)
         deinterleave(0, Q)
         transpose_x(0)
+        keep_warm(2)
         deinterleave(1, Q)
         quantise_weights(0)
         quantise_x(0)
         transpose_x(1)
+        keep_warm(2)
         quantise_x(1)
 
         for ob in range(O_BLOCKS):

@@ -13,16 +13,12 @@ ROWS = 1024
 IQ = 512
 OQ = 512
 ROW_TILES = ROWS // P
-PAIRS = ROW_TILES // 2
 O_BLOCKS = OQ // P
 MATRIX = P * 4
 BANK_BF16 = 1024
 BLOCK = 32
 BLOCKS = P // BLOCK
 MATMUL_COLS = 512
-DEINTERLEAVE_AT = 0
-TRANSPOSE_AT = 2
-SHARED = 2
 
 FLOPS = 2 * ROWS * IQ * OQ * 10
 
@@ -45,6 +41,9 @@ WEIGHT_FOR = (
 ROW_OF_BLOCKS = (NEG_WK, WR, WI, NEG_WI, WR, WJ, WK, NEG_WK, WK, NEG_WJ, NEG_WJ)
 SERVED = 2
 SLOTS = len(ROW_OF_BLOCKS)
+
+PLAIN_RUNS = ((1, 2), (5, 2), (4, 1), (8, 1))
+NEGATED_RUNS = ((0, 1), (3, 1), (7, 1), (9, 1), (10, 1))
 
 
 def slot_of(wanted):
@@ -69,6 +68,7 @@ def tile_quaternionlinear_pa_kernel(tc, x, wr, wi, wj, wk, bias, out):
         nc.scalar.copy(out=table_load[:], in_=ones[:, 0:1])
         bias_row = keep.tile([P, OQ * Q], BF16)
         nc.vector.memset(bias_row[:].bitcast(U32), 0)
+        nc.scalar.dma_start(out=bias_row[0:1, :], in_=bias.unsqueeze(0))
 
         w_raw = {}
         x_raw = {}
@@ -93,16 +93,13 @@ def tile_quaternionlinear_pa_kernel(tc, x, wr, wi, wj, wk, bias, out):
                 )
             x_raw[t] = rows
 
-        load_weights(0)
         load_x(0)
-        nc.sync.dma_start(out=bias_row[0:1, :], in_=bias.unsqueeze(0))
+        load_weights(0)
         load_x(1)
         for ob in range(1, O_BLOCKS):
             load_weights(ob)
         load_x(2)
-        load_x(3)
-        for t in range(4, ROW_TILES):
-            load_x_by_quarters(t)
+        load_x_by_quarters(3)
 
         identity = keep.tile([P, P], F32)
         make_identity(nc, identity[:])
@@ -114,6 +111,7 @@ def tile_quaternionlinear_pa_kernel(tc, x, wr, wi, wj, wk, bias, out):
         bias_all = keep.tile([P, OQ * Q], BF16)
         planes = {}
         x_grouped = {}
+        bias_banks = []
         accs = {}
         w_signed = {}
 
@@ -124,7 +122,8 @@ def tile_quaternionlinear_pa_kernel(tc, x, wr, wi, wj, wk, bias, out):
 
         def spread_bias():
             for b in range(OQ * Q // BANK_BF16):
-                bank = flipped.tile([P, BANK_BF16], BF16, tag="bank")
+                bank = sums.tile([P, BANK_BF16], BF16, tag="acc")
+                bias_banks.append(bank)
                 for h in range(BANK_BF16 // MATMUL_COLS):
                     nc.tensor.matmul(
                         out=bank[:, h * MATMUL_COLS : (h + 1) * MATMUL_COLS],
@@ -133,6 +132,9 @@ def tile_quaternionlinear_pa_kernel(tc, x, wr, wi, wj, wk, bias, out):
                         start=True,
                         stop=True,
                     )
+
+        def empty_bias():
+            for b, bank in enumerate(bias_banks):
                 nc.scalar.copy(out=bias_all[:, b * BANK_BF16 : (b + 1) * BANK_BF16], in_=bank[:])
 
         def transpose_and_group(words, grouped):
@@ -153,7 +155,7 @@ def tile_quaternionlinear_pa_kernel(tc, x, wr, wi, wj, wk, bias, out):
             )
             w_signed[ob] = signed
 
-        def quantise_weights(ob):
+        def negate_weights(ob):
             signed = w_signed[ob]
             nc.vector.tensor_scalar(
                 out=signed[:, NEG_WI * MATRIX :],
@@ -162,23 +164,30 @@ def tile_quaternionlinear_pa_kernel(tc, x, wr, wi, wj, wk, bias, out):
                 scalar2=None,
                 op0=mybir.AluOpType.mult,
             )
-            for negated in (False, True):
-                for s in range(SLOTS):
-                    which = ROW_OF_BLOCKS[s]
-                    if (which >= NEG_WI) == negated:
-                        nc.vector.quantize_mx(
-                            out=w_codes[:, ob, s * P : (s + 1) * P].bitcast(FP8X4),
-                            scales=w_scales[:, ob, s * P : (s + 1) * P],
-                            in_=signed[:, which * MATRIX : (which + 1) * MATRIX],
-                        )
+
+        def quantise_signed(ob, negated):
+            signed = w_signed[ob]
+            for s, n in NEGATED_RUNS if negated else PLAIN_RUNS:
+                which = ROW_OF_BLOCKS[s]
+                nc.vector.quantize_mx(
+                    out=w_codes[:, ob, s * P : (s + n) * P].bitcast(FP8X4),
+                    scales=w_scales[:, ob, s * P : (s + n) * P],
+                    in_=signed[:, which * MATRIX : (which + n) * MATRIX],
+                )
+
+        def quantise_weights(ob):
+            quantise_signed(ob, False)
+            negate_weights(ob)
+            quantise_signed(ob, True)
 
         def deinterleave(t, on_vector):
             separate = stage.tile([P, Q, 2, P, 2], BF16)
+            planes[t] = separate
             interleaved = x_raw[t][:].rearrange("r (p u e c) -> r c u p e", u=2, e=2, c=Q)
-            nc.vector.tensor_copy(out=separate[:, 0:on_vector], in_=interleaved[:, 0:on_vector])
+            if on_vector > 0:
+                nc.vector.tensor_copy(out=separate[:, 0:on_vector], in_=interleaved[:, 0:on_vector])
             if on_vector < Q:
                 nc.scalar.copy(out=separate[:, on_vector:Q], in_=interleaved[:, on_vector:Q])
-            planes[t] = separate
 
         def transpose_x(t):
             grouped = stage.tile([P, Q * MATRIX], BF16, align_bytes=64)
@@ -189,13 +198,13 @@ def tile_quaternionlinear_pa_kernel(tc, x, wr, wi, wj, wk, bias, out):
         def quantise_x(t):
             nc.vector.quantize_mx(out=x_codes[:, t, :].bitcast(FP8X4), scales=x_scales[:, t, :], in_=x_grouped[t][:])
 
-        def deinterleave_quarters(t):
-            blocks = stage.tile([P, BLOCKS, Q, 2, BLOCK, 2], BF16, align_bytes=64)
+        def deinterleave_quarters(t, components):
+            if t not in planes:
+                planes[t] = stage.tile([P, BLOCKS, Q, 2, BLOCK, 2], BF16, align_bytes=64, name="blocks")
             source = x_raw[t][:].rearrange("p n (a u e c) -> p c n u a e", u=2, e=2, c=Q)
-            target = blocks[:].rearrange("p n c u a e -> p c n u a e")
-            for c in range(Q):
+            target = planes[t][:].rearrange("p n c u a e -> p c n u a e")
+            for c in components:
                 nc.scalar.copy(out=target[:, c], in_=source[:, c])
-            planes[t] = blocks
 
         def transpose_blocks(t):
             turned = stage.tile([P, BLOCKS * Q * 2 * BLOCK], F32, align_bytes=64)
@@ -226,64 +235,75 @@ def tile_quaternionlinear_pa_kernel(tc, x, wr, wi, wj, wk, bias, out):
                         stop=(c_in == Q - 1),
                     )
 
-        def finish(t, ob):
-            acc = accs[t, ob]
-            cols = slice(ob * P * Q, (ob + 1) * P * Q)
-            result = results.tile([P, P * Q], F32)
-            nc.vector.tensor_tensor(
-                out=result[:].rearrange("p (o c) -> p o c", c=Q),
-                in0=acc[:].rearrange("p (c o) -> p o c", c=Q),
-                in1=bias_all[:, cols].rearrange("p (o c) -> p o c", c=Q),
-                op=mybir.AluOpType.add,
-            )
-            nc.sync.dma_start(out=out_rows[t * P : (t + 1) * P, cols], in_=result[:])
+        def finish(t, ob, pieces=1):
+            sums_by_quaternion = accs[t, ob][:].rearrange("p (c o) -> p o c", c=Q)
+            each = P // pieces
+            for i in range(pieces):
+                cols = slice((ob * P + i * each) * Q, (ob * P + (i + 1) * each) * Q)
+                result = results.tile([P, each * Q], F32, name="result%d" % pieces)
+                nc.vector.tensor_tensor(
+                    out=result[:].rearrange("p (o c) -> p o c", c=Q),
+                    in0=sums_by_quaternion[:, i * each : (i + 1) * each, :],
+                    in1=bias_all[:, cols].rearrange("p (o c) -> p o c", c=Q),
+                    op=mybir.AluOpType.add,
+                )
+                nc.sync.dma_start(out=out_rows[t * P : (t + 1) * P, cols], in_=result[:])
 
-        keep_warm(4)
+        keep_warm(7)
+        deinterleave(0, 2)
         transpose_weights(0)
-        keep_warm(6)
-        deinterleave(0, Q)
         transpose_x(0)
-        keep_warm(2)
-        deinterleave(1, Q)
-        quantise_weights(0)
+        spread_bias()
+        quantise_signed(0, False)
+        negate_weights(0)
         quantise_x(0)
+        quantise_signed(0, True)
+        transpose_weights(1)
+        deinterleave(1, 2)
+        multiply(0, 0)
         transpose_x(1)
-        keep_warm(2)
+        quantise_weights(1)
+        empty_bias()
+        transpose_weights(2)
+        multiply(0, 1)
         quantise_x(1)
+        multiply(1, 0)
+        finish(0, 0)
+        load_x_by_quarters(4)
+        multiply(1, 1)
+        quantise_weights(2)
+        deinterleave(2, 0)
+        finish(0, 1)
+        finish(1, 0)
+        transpose_weights(3)
+        multiply(0, 2)
+        transpose_x(2)
+        multiply(1, 2)
+        deinterleave_quarters(3, range(Q))
+        quantise_weights(3)
+        finish(1, 1)
+        finish(0, 2)
+        load_x_by_quarters(5)
+        quantise_x(2)
+        finish(1, 2)
+        multiply(0, 3)
+        multiply(1, 3)
+        finish(0, 3)
+        finish(1, 3)
 
-        for ob in range(O_BLOCKS):
-            if ob + 1 < O_BLOCKS:
-                transpose_weights(ob + 1)
-                quantise_weights(ob + 1)
-            for t in (2, 3):
-                if ob == DEINTERLEAVE_AT:
-                    deinterleave(t, SHARED)
-                if ob == TRANSPOSE_AT:
-                    transpose_x(t)
-                    quantise_x(t)
-            for t in (0, 1):
-                multiply(t, ob)
-            if ob == 0:
-                spread_bias()
-            for t in (0, 1):
-                finish(t, ob)
-
-        for pair in range(1, PAIRS):
-            a, b = 2 * pair + 2, 2 * pair + 3
-            ahead = (
-                ((deinterleave_quarters, a),),
-                ((deinterleave_quarters, b),),
-                (),
-                ((transpose_blocks, a),),
-                ((group_blocks, a),),
-                ((transpose_blocks, b),),
-                ((group_blocks, b), (quantise_x, a)),
-                ((quantise_x, b),),
-            )
+        for t in range(2, ROW_TILES):
             for ob in range(O_BLOCKS):
-                for t in (2 * pair, 2 * pair + 1):
-                    if pair + 1 < PAIRS:
-                        for step, tile in ahead[2 * ob + t % 2]:
-                            step(tile)
-                    multiply(t, ob)
-                    finish(t, ob)
+                if ob == 0 and t + 1 < ROW_TILES:
+                    transpose_blocks(t + 1)
+                if ob == 0 and t + 2 < ROW_TILES:
+                    deinterleave_quarters(t + 2, (0, 1))
+                if ob == 1 and t + 1 < ROW_TILES:
+                    group_blocks(t + 1)
+                if ob == 1 and t + 2 < ROW_TILES:
+                    deinterleave_quarters(t + 2, (2, 3))
+                if ob == 1 and 6 <= t + 4 < ROW_TILES:
+                    load_x_by_quarters(t + 4)
+                if ob == 2 and t + 1 < ROW_TILES:
+                    quantise_x(t + 1)
+                multiply(t, ob)
+                finish(t, ob, 2 if (t, ob) == (ROW_TILES - 1, O_BLOCKS - 1) else 1)

@@ -18,6 +18,7 @@ MATRIX = P * 4
 BANK_BF16 = 1024
 BLOCK = 32
 BLOCKS = P // BLOCK
+BY_SCALAR = 3
 MATMUL_COLS = 512
 
 FLOPS = 2 * ROWS * IQ * OQ * 10
@@ -249,6 +250,15 @@ def tile_quaternionlinear_pa_kernel(tc, x, wr, wi, wj, wk, bias, out):
                 )
                 nc.sync.dma_start(out=out_rows[t * P : (t + 1) * P, cols], in_=result[:])
 
+        def finish_by_scalar(t, ob):
+            cols = slice(ob * P * Q, (ob + 1) * P * Q)
+            result = results.tile([P, P * Q], F32, name="result1")
+            nc.scalar.copy(
+                out=result[:].rearrange("p (o c) -> p o c", c=Q), in_=accs[t, ob][:].rearrange("p (c o) -> p o c", c=Q)
+            )
+            nc.gpsimd.tensor_tensor(out=result[:], in0=result[:], in1=bias_all[:, cols], op=mybir.AluOpType.add)
+            nc.sync.dma_start(out=out_rows[t * P : (t + 1) * P, cols], in_=result[:])
+
         keep_warm(7)
         deinterleave(0, 2)
         transpose_weights(0)
@@ -306,4 +316,7 @@ def tile_quaternionlinear_pa_kernel(tc, x, wr, wi, wj, wk, bias, out):
                 if ob == 2 and t + 1 < ROW_TILES:
                     quantise_x(t + 1)
                 multiply(t, ob)
-                finish(t, ob, 2 if (t, ob) == (ROW_TILES - 1, O_BLOCKS - 1) else 1)
+                if ob == BY_SCALAR and t + 1 < ROW_TILES:
+                    finish_by_scalar(t, ob)
+                else:
+                    finish(t, ob, 2 if (t, ob) == (ROW_TILES - 1, O_BLOCKS - 1) else 1)

@@ -23,13 +23,13 @@ MATMUL_COLS = 512
 
 FLOPS = 2 * ROWS * IQ * OQ * 10
 
-WR = 0
-WI = 1
-WJ = 2
-WK = 3
+WI = 0
+WK = 1
+WR = 2
+WJ = 3
 NEG_WI = 4
-NEG_WJ = 5
-NEG_WK = 6
+NEG_WK = 5
+NEG_WJ = 6
 SIGNED = 7
 
 WEIGHT_FOR = (
@@ -39,17 +39,20 @@ WEIGHT_FOR = (
     (WK, NEG_WI, WJ, WR),
 )
 
-ROW_OF_BLOCKS = (NEG_WK, WR, WI, NEG_WI, WR, WJ, WK, NEG_WK, WK, NEG_WJ, NEG_WJ)
-SERVED = 2
+BANK_ORDER = (1, 3, 0, 2)
+
+ROW_OF_BLOCKS = (NEG_WJ, WJ, NEG_WJ, WR, NEG_WI, WI, WK, WR, WJ, NEG_WK, NEG_WK)
 SLOTS = len(ROW_OF_BLOCKS)
 
-PLAIN_RUNS = ((1, 2), (5, 2), (4, 1), (8, 1))
-NEGATED_RUNS = ((0, 1), (3, 1), (7, 1), (9, 1), (10, 1))
+PLAIN_RUNS = ((5, 2), (7, 2), (3, 1), (1, 1))
+NEGATED_RUNS = ((4, 1), (9, 1), (10, 1), (0, 1), (2, 1))
+
+PASSES = ((0, 0, 4), (2, 0, 4), (1, 0, 2), (1, 2, 2), (3, 0, 2), (3, 2, 2))
 
 
 def slot_of(wanted):
-    for s in range(SLOTS - SERVED + 1):
-        if ROW_OF_BLOCKS[s : s + SERVED] == wanted:
+    for s in range(SLOTS - len(wanted) + 1):
+        if ROW_OF_BLOCKS[s : s + len(wanted)] == wanted:
             return s
     raise AssertionError("these weights are not neighbours in ROW_OF_BLOCKS")
 
@@ -58,7 +61,7 @@ def tile_quaternionlinear_pa_kernel(tc, x, wr, wi, wj, wk, bias, out):
     nc = tc.nc
     x_rows = x.flatten_outer_dims()
     out_rows = out.flatten_outer_dims()
-    weights = (wr, wi, wj, wk)
+    weights = (wi, wk, wr, wj)
 
     with tc.tile_pool(name="keep", bufs=1) as keep, tc.tile_pool(name="stage", bufs=4) as stage, tc.tile_pool(
         name="results", bufs=8
@@ -158,13 +161,14 @@ def tile_quaternionlinear_pa_kernel(tc, x, wr, wi, wj, wk, bias, out):
 
         def negate_weights(ob):
             signed = w_signed[ob]
-            nc.vector.tensor_scalar(
-                out=signed[:, NEG_WI * MATRIX :],
-                in0=signed[:, WI * MATRIX : Q * MATRIX],
-                scalar1=-1.0,
-                scalar2=None,
-                op0=mybir.AluOpType.mult,
-            )
+            for negative, positive, n in ((NEG_WI, WI, 2), (NEG_WJ, WJ, 1)):
+                nc.vector.tensor_scalar(
+                    out=signed[:, negative * MATRIX : (negative + n) * MATRIX],
+                    in0=signed[:, positive * MATRIX : (positive + n) * MATRIX],
+                    scalar1=-1.0,
+                    scalar2=None,
+                    op0=mybir.AluOpType.mult,
+                )
 
         def quantise_signed(ob, negated):
             signed = w_signed[ob]
@@ -223,29 +227,31 @@ def tile_quaternionlinear_pa_kernel(tc, x, wr, wi, wj, wk, bias, out):
         def multiply(t, ob):
             acc = sums.tile([P, Q * P], F32, tag="acc")
             accs[t, ob] = acc
-            for first in range(0, Q, SERVED):
-                for c_in in range(Q):
-                    s = slot_of(tuple(WEIGHT_FOR[c_out][c_in] for c_out in range(first, first + SERVED)))
-                    nc.tensor.matmul_mx(
-                        out=acc[:, first * P : (first + SERVED) * P],
-                        lhsT=x_codes[:, t, c_in * P : (c_in + 1) * P].bitcast(FP8X4),
-                        lhsT_scale=x_scales[:, t, c_in * P : (c_in + 1) * P],
-                        rhs=w_codes[:, ob, s * P : (s + SERVED) * P].bitcast(FP8X4),
-                        rhs_scale=w_scales[:, ob, s * P : (s + SERVED) * P],
-                        start=(c_in == 0),
-                        stop=(c_in == Q - 1),
-                    )
+            for i, (c_in, first, served) in enumerate(PASSES):
+                s = slot_of(tuple(WEIGHT_FOR[c_out][c_in] for c_out in BANK_ORDER[first : first + served]))
+                nc.tensor.matmul_mx(
+                    out=acc[:, first * P : (first + served) * P],
+                    lhsT=x_codes[:, t, c_in * P : (c_in + 1) * P].bitcast(FP8X4),
+                    lhsT_scale=x_scales[:, t, c_in * P : (c_in + 1) * P],
+                    rhs=w_codes[:, ob, s * P : (s + served) * P].bitcast(FP8X4),
+                    rhs_scale=w_scales[:, ob, s * P : (s + served) * P],
+                    start=(i == 0),
+                    stop=(i == len(PASSES) - 1),
+                )
+
+        def by_quaternion(acc):
+            return acc[:].rearrange("p (h s o) -> p o s h", h=2, s=2)[:, :, :, ::-1]
 
         def finish(t, ob, pieces=1):
-            sums_by_quaternion = accs[t, ob][:].rearrange("p (c o) -> p o c", c=Q)
+            quaternions = by_quaternion(accs[t, ob])
             each = P // pieces
             for i in range(pieces):
                 cols = slice((ob * P + i * each) * Q, (ob * P + (i + 1) * each) * Q)
                 result = results.tile([P, each * Q], F32, name="result%d" % pieces)
                 nc.vector.tensor_tensor(
-                    out=result[:].rearrange("p (o c) -> p o c", c=Q),
-                    in0=sums_by_quaternion[:, i * each : (i + 1) * each, :],
-                    in1=bias_all[:, cols].rearrange("p (o c) -> p o c", c=Q),
+                    out=result[:].rearrange("p (o s e) -> p o s e", s=2, e=2),
+                    in0=quaternions[:, i * each : (i + 1) * each],
+                    in1=bias_all[:, cols].rearrange("p (o s e) -> p o s e", s=2, e=2),
                     op=mybir.AluOpType.add,
                 )
                 nc.sync.dma_start(out=out_rows[t * P : (t + 1) * P, cols], in_=result[:])
@@ -254,7 +260,7 @@ def tile_quaternionlinear_pa_kernel(tc, x, wr, wi, wj, wk, bias, out):
             cols = slice(ob * P * Q, (ob + 1) * P * Q)
             result = results.tile([P, P * Q], F32, name="result1")
             nc.scalar.copy(
-                out=result[:].rearrange("p (o c) -> p o c", c=Q), in_=accs[t, ob][:].rearrange("p (c o) -> p o c", c=Q)
+                out=result[:].rearrange("p (o s e) -> p o s e", s=2, e=2), in_=by_quaternion(accs[t, ob])
             )
             nc.gpsimd.tensor_tensor(out=result[:], in0=result[:], in1=bias_all[:, cols], op=mybir.AluOpType.add)
             nc.sync.dma_start(out=out_rows[t * P : (t + 1) * P, cols], in_=result[:])

@@ -108,10 +108,10 @@ def tile_quaternionlinear_pa_kernel(tc, x, wr, wi, wj, wk, bias, out):
         identity = keep.tile([P, P], F32)
         make_identity(nc, identity[:])
 
-        w_codes = keep.tile([P, O_BLOCKS, SLOTS * P], U32, align_bytes=64)
-        w_scales = keep.tile([P, O_BLOCKS, SLOTS * P], U8, align_bytes=64)
-        x_codes = keep.tile([P, ROW_TILES, Q * P], U32, align_bytes=64)
-        x_scales = keep.tile([P, ROW_TILES, Q * P], U8, align_bytes=64)
+        w_codes = keep.tile([P, O_BLOCKS, SLOTS * P], U32, align_bytes=256)
+        w_scales = keep.tile([P, O_BLOCKS, SLOTS * P], U8, align_bytes=256)
+        x_codes = keep.tile([P, ROW_TILES, Q * P], U32, align_bytes=256)
+        x_scales = keep.tile([P, ROW_TILES, Q * P], U8, align_bytes=256)
         bias_all = keep.tile([P, OQ * Q], BF16)
         planes = {}
         x_grouped = {}

@@ -47,7 +47,7 @@ SLOTS = len(ROW_OF_BLOCKS)
 PLAIN_RUNS = ((5, 2), (7, 2), (3, 1), (1, 1))
 NEGATED_RUNS = ((4, 1), (9, 1), (10, 1), (0, 1), (2, 1))
 
-PASSES = ((0, 0, 4), (2, 0, 4), (1, 0, 2), (1, 2, 2), (3, 0, 2), (3, 2, 2))
+PASSES = ((0, 0, 4), (1, 0, 2), (1, 2, 2), (3, 0, 2), (3, 2, 2), (2, 0, 4))
 
 
 def slot_of(wanted):
@@ -292,8 +292,8 @@ def tile_quaternionlinear_pa_kernel(tc, x, wr, wi, wj, wk, bias, out):
         finish(0, 1)
         finish(1, 0)
         transpose_weights(3)
-        multiply(0, 2)
         transpose_x(2)
+        multiply(0, 2)
         multiply(1, 2)
         deinterleave_quarters(3, range(Q))
         quantise_weights(3)
@@ -304,8 +304,8 @@ def tile_quaternionlinear_pa_kernel(tc, x, wr, wi, wj, wk, bias, out):
         finish(1, 2)
         multiply(0, 3)
         multiply(1, 3)
-        finish(0, 3)
-        finish(1, 3)
+        finish_by_scalar(0, 3)
+        finish_by_scalar(1, 3)
 
         for t in range(2, ROW_TILES):
             for ob in range(O_BLOCKS):
@@ -325,4 +325,4 @@ def tile_quaternionlinear_pa_kernel(tc, x, wr, wi, wj, wk, bias, out):
                 if ob == BY_SCALAR and t + 1 < ROW_TILES:
                     finish_by_scalar(t, ob)
                 else:
-                    finish(t, ob, 2 if (t, ob) == (ROW_TILES - 1, O_BLOCKS - 1) else 1)
+                    finish(t, ob, 4 if (t, ob) == (ROW_TILES - 1, O_BLOCKS - 1) else 1)

@@ -64,7 +64,7 @@ def tile_quaternionlinear_pa_kernel(tc, x, wr, wi, wj, wk, bias, out):
     weights = (wi, wk, wr, wj)
 
     with tc.tile_pool(name="keep", bufs=1) as keep, tc.tile_pool(name="stage", bufs=4) as stage, tc.tile_pool(
-        name="results", bufs=8
+        name="results", bufs=12
     ) as results, tc.psum_pool(name="flipped", bufs=4) as flipped, tc.psum_pool(name="sums", bufs=4) as sums, tc.manual_schedule():
         ones = keep.tile([P, MATMUL_COLS], BF16)
         nc.vector.memset(ones[:], 1.0)
@@ -104,6 +104,7 @@ def tile_quaternionlinear_pa_kernel(tc, x, wr, wi, wj, wk, bias, out):
             load_weights(ob)
         load_x(2)
         load_x_by_quarters(3)
+        load_x_by_quarters(4)
 
         identity = keep.tile([P, P], F32)
         make_identity(nc, identity[:])
@@ -285,7 +286,7 @@ def tile_quaternionlinear_pa_kernel(tc, x, wr, wi, wj, wk, bias, out):
         quantise_x(1)
         multiply(1, 0)
         finish(0, 0)
-        load_x_by_quarters(4)
+        load_x_by_quarters(5)
         multiply(1, 1)
         quantise_weights(2)
         deinterleave(2, 0)
@@ -299,12 +300,13 @@ def tile_quaternionlinear_pa_kernel(tc, x, wr, wi, wj, wk, bias, out):
         quantise_weights(3)
         finish(1, 1)
         finish(0, 2)
-        load_x_by_quarters(5)
+        load_x_by_quarters(6)
         quantise_x(2)
         finish(1, 2)
         multiply(0, 3)
         multiply(1, 3)
         finish_by_scalar(0, 3)
+        load_x_by_quarters(7)
         finish_by_scalar(1, 3)
 
         for t in range(2, ROW_TILES):
@@ -317,8 +319,6 @@ def tile_quaternionlinear_pa_kernel(tc, x, wr, wi, wj, wk, bias, out):
                     group_blocks(t + 1)
                 if ob == 1 and t + 2 < ROW_TILES:
                     deinterleave_quarters(t + 2, (2, 3))
-                if ob == 1 and 6 <= t + 4 < ROW_TILES:
-                    load_x_by_quarters(t + 4)
                 if ob == 2 and t + 1 < ROW_TILES:
                     quantise_x(t + 1)
                 multiply(t, ob)

import concourse.mybir as mybir
from concourse.masks import make_identity

F32 = mybir.dt.float32
BF16 = mybir.dt.bfloat16
U32 = mybir.dt.uint32
U8 = mybir.dt.uint8
FP8X4 = mybir.dt.float8_e4m3fn_x4

P = 128
Q = 4
ROWS = 1024
IQ = 512
OQ = 512
ROW_TILES = ROWS // P
O_BLOCKS = OQ // P
MATRIX = P * 4
BANK_BF16 = 1024
BLOCK = 32
BLOCKS = P // BLOCK
BY_SCALAR = 3
MATMUL_COLS = 512

FLOPS = 2 * ROWS * IQ * OQ * 10

WI = 0
WK = 1
WR = 2
WJ = 3
NEG_WI = 4
NEG_WK = 5
NEG_WJ = 6
SIGNED = 7

WEIGHT_FOR = (
    (WR, NEG_WI, NEG_WJ, NEG_WK),
    (WI, WR, NEG_WJ, WK),
    (WJ, WI, WR, NEG_WK),
    (WK, NEG_WI, WJ, WR),
)

BANK_ORDER = (1, 3, 0, 2)

ROW_OF_BLOCKS = (NEG_WJ, WJ, NEG_WJ, WR, NEG_WI, WI, WK, WR, WJ, NEG_WK, NEG_WK)
SLOTS = len(ROW_OF_BLOCKS)

PLAIN_RUNS = ((5, 2), (7, 2), (3, 1), (1, 1))
NEGATED_RUNS = ((4, 1), (9, 1), (10, 1), (0, 1), (2, 1))

PASSES = ((0, 0, 4), (1, 0, 2), (1, 2, 2), (3, 0, 2), (3, 2, 2), (2, 0, 4))


def slot_of(wanted):
    for s in range(SLOTS - len(wanted) + 1):
        if ROW_OF_BLOCKS[s : s + len(wanted)] == wanted:
            return s
    raise AssertionError("these weights are not neighbours in ROW_OF_BLOCKS")


def tile_quaternionlinear_pa_kernel(tc, x, wr, wi, wj, wk, bias, out):
    nc = tc.nc
    x_rows = x.flatten_outer_dims()
    out_rows = out.flatten_outer_dims()
    weights = (wi, wk, wr, wj)

    with tc.tile_pool(name="keep", bufs=1) as keep, tc.tile_pool(name="stage", bufs=4) as stage, tc.tile_pool(
        name="results", bufs=12
    ) as results, tc.psum_pool(name="flipped", bufs=4) as flipped, tc.psum_pool(name="sums", bufs=4) as sums, tc.manual_schedule():
        ones = keep.tile([P, MATMUL_COLS], BF16)
        nc.vector.memset(ones[:], 1.0)
        table_load = keep.tile([P, 1], BF16)
        nc.scalar.copy(out=table_load[:], in_=ones[:, 0:1])
        bias_row = keep.tile([P, OQ * Q], BF16)
        nc.vector.memset(bias_row[:].bitcast(U32), 0)
        nc.scalar.dma_start(out=bias_row[0:1, :], in_=bias.unsqueeze(0))

        w_raw = {}
        x_raw = {}

        def load_weights(ob):
            block = keep.tile([P, Q, IQ], BF16, name="w_raw%d" % ob)
            for m in range(Q):
                nc.sync.dma_start(out=block[:, m, :], in_=weights[m][ob * P : (ob + 1) * P, :])
            w_raw[ob] = block

        def load_x(t):
            rows = keep.tile([P, IQ * Q], BF16, name="x_raw%d" % t)
            nc.sync.dma_start(out=rows[:], in_=x_rows[t * P : (t + 1) * P, :])
            x_raw[t] = rows

        def load_x_by_quarters(t):
            rows = keep.tile([P, BLOCKS, IQ], BF16, name="x_raw%d" % t)
            for q in (0, 2, 1, 3):
                nc.sync.dma_start(
                    out=rows[q * BLOCK : (q + 1) * BLOCK, :, :],
                    in_=x_rows[t * P : (t + 1) * P, q * IQ : (q + 1) * IQ].rearrange("(n r) w -> r n w", n=BLOCKS),
                )
            x_raw[t] = rows

        load_x(0)
        load_weights(0)
        load_x(1)
        for ob in range(1, O_BLOCKS):
            load_weights(ob)
        load_x(2)
        load_x_by_quarters(3)
        load_x_by_quarters(4)

        identity = keep.tile([P, P], F32)
        make_identity(nc, identity[:])

        w_codes = keep.tile([P, O_BLOCKS, SLOTS * P], U32, align_bytes=256)
        w_scales = keep.tile([P, O_BLOCKS, SLOTS * P], U8, align_bytes=256)
        x_codes = keep.tile([P, ROW_TILES, Q * P], U32, align_bytes=256)
        x_scales = keep.tile([P, ROW_TILES, Q * P], U8, align_bytes=256)
        bias_all = keep.tile([P, OQ * Q], BF16)
        planes = {}
        x_grouped = {}
        bias_banks = []
        accs = {}
        w_signed = {}

        def keep_warm(n):
            unread = sums.tile([P, MATMUL_COLS], F32, tag="acc")
            for i in range(n):
                nc.tensor.matmul(out=unread[:], lhsT=ones[:, 0:P], rhs=ones[:], start=True, stop=True)

        def spread_bias():
            for b in range(OQ * Q // BANK_BF16):
                bank = sums.tile([P, BANK_BF16], BF16, tag="acc")
                bias_banks.append(bank)
                for h in range(BANK_BF16 // MATMUL_COLS):
                    nc.tensor.matmul(
                        out=bank[:, h * MATMUL_COLS : (h + 1) * MATMUL_COLS],
                        lhsT=ones[:, 0:P],
                        rhs=bias_row[:, b * BANK_BF16 + h * MATMUL_COLS : b * BANK_BF16 + (h + 1) * MATMUL_COLS],
                        start=True,
                        stop=True,
                    )

        def empty_bias():
            for b, bank in enumerate(bias_banks):
                nc.scalar.copy(out=bias_all[:, b * BANK_BF16 : (b + 1) * BANK_BF16], in_=bank[:])

        def transpose_and_group(words, grouped):
            grouped_words = grouped.bitcast(F32).rearrange("p (m r u) -> p m r u", m=Q, u=2)
            for pair in range(2):
                bank = flipped.tile([P, 2, 2, P], F32, tag="bank")
                for m in range(2):
                    for u in range(2):
                        nc.tensor.transpose(bank[:, m, u, :], words[:, 2 * pair + m, u, :], identity[:])
                nc.scalar.copy(
                    out=grouped_words[:, 2 * pair : 2 * pair + 2, :, :], in_=bank[:].rearrange("p m u r -> p m r u")
                )

        def transpose_weights(ob):
            signed = stage.tile([P, SIGNED * MATRIX], BF16, align_bytes=64)
            transpose_and_group(
                w_raw[ob][:].bitcast(F32).rearrange("r m (p u) -> r m u p", u=2), signed[:, 0 : Q * MATRIX]
            )
            w_signed[ob] = signed

        def negate_weights(ob):
            signed = w_signed[ob]
            for negative, positive, n in ((NEG_WI, WI, 2), (NEG_WJ, WJ, 1)):
                nc.vector.tensor_scalar(
                    out=signed[:, negative * MATRIX : (negative + n) * MATRIX],
                    in0=signed[:, positive * MATRIX : (positive + n) * MATRIX],
                    scalar1=-1.0,
                    scalar2=None,
                    op0=mybir.AluOpType.mult,
                )

        def quantise_signed(ob, negated):
            signed = w_signed[ob]
            for s, n in NEGATED_RUNS if negated else PLAIN_RUNS:
                which = ROW_OF_BLOCKS[s]
                nc.vector.quantize_mx(
                    out=w_codes[:, ob, s * P : (s + n) * P].bitcast(FP8X4),
                    scales=w_scales[:, ob, s * P : (s + n) * P],
                    in_=signed[:, which * MATRIX : (which + n) * MATRIX],
                )

        def quantise_weights(ob):
            quantise_signed(ob, False)
            negate_weights(ob)
            quantise_signed(ob, True)

        def deinterleave(t, on_vector):
            separate = stage.tile([P, Q, 2, P, 2], BF16)
            planes[t] = separate
            interleaved = x_raw[t][:].rearrange("r (p u e c) -> r c u p e", u=2, e=2, c=Q)
            if on_vector > 0:
                nc.vector.tensor_copy(out=separate[:, 0:on_vector], in_=interleaved[:, 0:on_vector])
            if on_vector < Q:
                nc.scalar.copy(out=separate[:, on_vector:Q], in_=interleaved[:, on_vector:Q])

        def transpose_x(t):
            grouped = stage.tile([P, Q * MATRIX], BF16, align_bytes=64)
            words = planes[t][:].rearrange("r m u p e -> r m (u p e)").bitcast(F32)
            transpose_and_group(words.rearrange("r m (u p) -> r m u p", u=2), grouped[:])
            x_grouped[t] = grouped

        def quantise_x(t):
            nc.vector.quantize_mx(out=x_codes[:, t, :].bitcast(FP8X4), scales=x_scales[:, t, :], in_=x_grouped[t][:])

        def deinterleave_quarters(t, components):
            if t not in planes:
                planes[t] = stage.tile([P, BLOCKS, Q, 2, BLOCK, 2], BF16, align_bytes=64, name="blocks")
            source = x_raw[t][:].rearrange("p n (a u e c) -> p c n u a e", u=2, e=2, c=Q)
            target = planes[t][:].rearrange("p n c u a e -> p c n u a e")
            for c in components:
                nc.scalar.copy(out=target[:, c], in_=source[:, c])

        def transpose_blocks(t):
            turned = stage.tile([P, BLOCKS * Q * 2 * BLOCK], F32, align_bytes=64)
            nc.vector.transpose(turned[:], planes[t][:].rearrange("p n c u a e -> p (n c u a e)").bitcast(F32))
            planes[t] = turned

        def group_blocks(t):
            grouped = stage.tile([P, Q * MATRIX], BF16, align_bytes=64)
            nc.scalar.copy(
                out=grouped[:].bitcast(F32).rearrange("p (c n r u) -> p c n r u", c=Q, n=BLOCKS, u=2),
                in_=planes[t][:].rearrange("p (n c u r) -> p c n r u", n=BLOCKS, c=Q, u=2),
            )
            x_grouped[t] = grouped

        def multiply(t, ob):
            acc = sums.tile([P, Q * P], F32, tag="acc")
            accs[t, ob] = acc
            for i, (c_in, first, served) in enumerate(PASSES):
                s = slot_of(tuple(WEIGHT_FOR[c_out][c_in] for c_out in BANK_ORDER[first : first + served]))
                nc.tensor.matmul_mx(
                    out=acc[:, first * P : (first + served) * P],
                    lhsT=x_codes[:, t, c_in * P : (c_in + 1) * P].bitcast(FP8X4),
                    lhsT_scale=x_scales[:, t, c_in * P : (c_in + 1) * P],
                    rhs=w_codes[:, ob, s * P : (s + served) * P].bitcast(FP8X4),
                    rhs_scale=w_scales[:, ob, s * P : (s + served) * P],
                    start=(i == 0),
                    stop=(i == len(PASSES) - 1),
                )

        def by_quaternion(acc):
            return acc[:].rearrange("p (h s o) -> p o s h", h=2, s=2)[:, :, :, ::-1]

        def finish(t, ob, pieces=1):
            quaternions = by_quaternion(accs[t, ob])
            each = P // pieces
            for i in range(pieces):
                cols = slice((ob * P + i * each) * Q, (ob * P + (i + 1) * each) * Q)
                result = results.tile([P, each * Q], F32, name="result%d" % pieces)
                nc.vector.tensor_tensor(
                    out=result[:].rearrange("p (o s e) -> p o s e", s=2, e=2),
                    in0=quaternions[:, i * each : (i + 1) * each],
                    in1=bias_all[:, cols].rearrange("p (o s e) -> p o s e", s=2, e=2),
                    op=mybir.AluOpType.add,
                )
                nc.sync.dma_start(out=out_rows[t * P : (t + 1) * P, cols], in_=result[:])

        def finish_by_scalar(t, ob):
            cols = slice(ob * P * Q, (ob + 1) * P * Q)
            result = results.tile([P, P * Q], F32, name="result1")
            nc.scalar.copy(
                out=result[:].rearrange("p (o s e) -> p o s e", s=2, e=2), in_=by_quaternion(accs[t, ob])
            )
            nc.gpsimd.tensor_tensor(out=result[:], in0=result[:], in1=bias_all[:, cols], op=mybir.AluOpType.add)
            nc.sync.dma_start(out=out_rows[t * P : (t + 1) * P, cols], in_=result[:])

        keep_warm(7)
        deinterleave(0, 2)
        transpose_weights(0)
        transpose_x(0)
        spread_bias()
        quantise_signed(0, False)
        negate_weights(0)
        quantise_x(0)
        quantise_signed(0, True)
        transpose_weights(1)
        deinterleave(1, 2)
        multiply(0, 0)
        transpose_x(1)
        quantise_weights(1)
        empty_bias()
        transpose_weights(2)
        multiply(0, 1)
        quantise_x(1)
        multiply(1, 0)
        finish(0, 0)
        load_x_by_quarters(5)
        multiply(1, 1)
        quantise_weights(2)
        deinterleave(2, 0)
        finish(0, 1)
        finish(1, 0)
        transpose_weights(3)
        transpose_x(2)
        multiply(0, 2)
        multiply(1, 2)
        deinterleave_quarters(3, range(Q))
        quantise_weights(3)
        finish(1, 1)
        finish(0, 2)
        load_x_by_quarters(6)
        quantise_x(2)
        finish(1, 2)
        multiply(0, 3)
        multiply(1, 3)
        finish_by_scalar(0, 3)
        load_x_by_quarters(7)
        finish_by_scalar(1, 3)

        for t in range(2, ROW_TILES):
            for ob in range(O_BLOCKS):
                if ob == 0 and t + 1 < ROW_TILES:
                    transpose_blocks(t + 1)
                if ob == 0 and t + 2 < ROW_TILES:
                    deinterleave_quarters(t + 2, (0, 1))
                if ob == 1 and t + 1 < ROW_TILES:
                    group_blocks(t + 1)
                if ob == 1 and t + 2 < ROW_TILES:
                    deinterleave_quarters(t + 2, (2, 3))
                if ob == 2 and t + 1 < ROW_TILES:
                    quantise_x(t + 1)
                multiply(t, ob)
                if ob == BY_SCALAR and t + 1 < ROW_TILES:
                    finish_by_scalar(t, ob)
                else:
                    finish(t, ob, 4 if (t, ob) == (ROW_TILES - 1, O_BLOCKS - 1) else 1)
